import numpy as np
import ml_dtypes

BF16 = ml_dtypes.bfloat16


def bf(x):
    return np.asarray(x, np.float32).astype(BF16)


def f32(x):
    return np.asarray(x, np.float32)


def f64(x):
    return np.asarray(x).astype(np.float64)


def striped(idx):
    return np.tile(idx.reshape(-1, 16).T, (8, 1))


F, C, S, N = 512, 512, 2048, 512
LN_EPS = 1e-5


def setup_inputs():
    return {"x": bf(np.random.standard_normal((F, N))), "w": bf(np.random.standard_normal((F, C)) / np.sqrt(F)), "b": f32(0.1 * np.random.standard_normal((C, 1))), "gain": f32(1.0 + 0.1 * np.random.standard_normal((C, 1))), "beta": f32(0.1 * np.random.standard_normal((C, 1))), "base": f32(np.random.standard_normal((C, S))), "offs": striped(np.random.permutation(S)[:N])}


def reference(x, w, b, gain, beta, base, offs):
    idx = offs[:16].T.reshape(-1)
    h = np.maximum(f64(w).T @ f64(x) + f64(b), 0.0)
    mu = h.mean(axis=0, keepdims=True)
    var = np.square(h - mu).mean(axis=0, keepdims=True)
    res = f64(base).copy()
    res[:, idx] = (h - mu) / np.sqrt(var + LN_EPS) * f64(gain) + f64(beta)
    return res

@@ -1,0 +1,98 @@
+import concourse.mybir as mybir
+from concourse.masks import make_identity
+
+P = 128
+F, C, S, N = 512, 512, 2048, 512
+FB, CB, JB = F // P, C // P, N // P
+LN_EPS = 1e-5
+FLOPS = 2 * F * C * N
+
+BF16, F32, U16 = mybir.dt.bfloat16, mybir.dt.float32, mybir.dt.uint16
+ADD, SUBTRACT, MULT = mybir.AluOpType.add, mybir.AluOpType.subtract, mybir.AluOpType.mult
+ACT = mybir.ActivationFunctionType
+
+
+def tile_semanticgraphnetwork_kernel(tc, x, w, b, gain, beta, base, offs, out):
+    nc = tc.nc
+    with (
+        tc.tile_pool(name="held", bufs=1) as held,
+        tc.tile_pool(name="work", bufs=2) as work,
+        tc.tile_pool(name="stat", bufs=4) as stat,
+        tc.psum_pool(name="psum_z", bufs=2) as psum_z,
+        tc.psum_pool(name="psum_t", bufs=2) as psum_t,
+        tc.psum_pool(name="psum_cols", bufs=1) as psum_cols,
+    ):
+        offsets = held.tile([P, N // 16], U16, name="offsets")
+        nc.sync.dma_start(offsets[:], offs)
+
+        x_blocks = x.rearrange("(fb p) j -> fb p j", p=P)
+        w_blocks = w.rearrange("(fb p) c -> fb p c", p=P)
+        x_sb = [held.tile([P, N], BF16, name=f"x{fb}") for fb in range(FB)]
+        w_sb = [held.tile([P, C], BF16, name=f"w{fb}") for fb in range(FB)]
+        for fb in range(FB):
+            nc.sync.dma_start(x_sb[fb][:], x_blocks[fb])
+            nc.scalar.dma_start(w_sb[fb][:], w_blocks[fb])
+
+        b_rows = held.tile([P, C], F32, name="b_rows")
+        nc.gpsimd.dma_start(b_rows[:], b.rearrange("c one -> (c one)").partition_broadcast(P))
+
+        rows = held.tile([P, P], F32, name="rows")
+        nc.vector.memset(rows[:], 0.0)
+        nc.gpsimd.dma_start(rows[0:CB, :], gain.rearrange("(cb p) one -> cb (p one)", p=P))
+        nc.gpsimd.dma_start(rows[CB : 2 * CB, :], beta.rearrange("(cb p) one -> cb (p one)", p=P))
+
+        base_blocks = base.rearrange("(cb p) s -> cb p s", p=P)
+        out_blocks = out.rearrange("(cb p) s -> cb p s", p=P)
+        window = [held.tile([P, S], F32, name=f"window{cb}") for cb in range(CB)]
+        for cb in range(CB):
+            queue = nc.sync if cb % 2 == 0 else nc.scalar
+            queue.dma_start(window[cb][:], base_blocks[cb])
+
+        identity = held.tile([P, P], F32, name="identity")
+        make_identity(nc, identity[:])
+        eps = held.tile([P, 1], F32, name="eps")
+        nc.vector.memset(eps[:], LN_EPS)
+
+        rows_flipped = psum_cols.tile([P, P], F32, name="rows_flipped")
+        nc.tensor.transpose(rows_flipped[:], rows[:], identity[:])
+        per_channel = held.tile([P, 2 * CB], F32, name="per_channel")
+        nc.vector.tensor_copy(per_channel[:], rows_flipped[:, 0 : 2 * CB])
+
+        zeros = held.tile([P, N], F32, name="zeros")
+        nc.gpsimd.memset(zeros[:], 0.0)
+        beta_wide = [held.tile([P, N], F32, name=f"beta_wide{cb}") for cb in range(CB)]
+        for cb in range(CB):
+            nc.gpsimd.tensor_scalar(beta_wide[cb][:], zeros[:], per_channel[:, CB + cb : CB + cb + 1], None, ADD)
+
+        normed = [held.tile([P, C], F32, name=f"normed{jb}") for jb in range(JB)]
+        for jb in range(JB):
+            z = psum_z.tile([P, C], F32, name="z")
+            for fb in range(FB):
+                nc.tensor.matmul(
+                    z[:], x_sb[fb][:, jb * P : (jb + 1) * P], w_sb[fb][:], start=(fb == 0), stop=(fb == FB - 1)
+                )
+            biased = work.tile([P, C], F32, name="biased")
+            nc.vector.tensor_tensor(biased[:], z[:], b_rows[:], ADD)
+            h = work.tile([P, C], F32, name="h")
+            nc.scalar.activation(h[:], biased[:], ACT.Relu)
+
+            six = stat.tile([P, 6], F32, name="six")
+            nc.vector.bn_stats(six[:], h[:])
+            mean_var = stat.tile([P, 2], F32, name="mean_var")
+            nc.vector.bn_aggr(mean_var[:], six[:])
+            std = stat.tile([P, 1], F32, name="std")
+            nc.scalar.activation(std[:], mean_var[:, 1:2], ACT.Sqrt, bias=eps[:])
+            rstd = stat.tile([P, 1], F32, name="rstd")
+            nc.vector.reciprocal(rstd[:], std[:])
+            nc.vector.tensor_scalar(normed[jb][:], h[:], mean_var[:, 0:1], rstd[:], SUBTRACT, MULT)
+
+        for cb in range(CB):
+            flipped = psum_t.tile([P, N], F32, name="flipped")
+            for jb in range(JB):
+                nc.tensor.transpose(
+                    flipped[:, jb * P : (jb + 1) * P], normed[jb][:, cb * P : (cb + 1) * P], identity[:]
+                )
+            scaled = work.tile([P, N], F32, name="scaled")
+            nc.scalar.activation(scaled[:], flipped[:], ACT.Identity, scale=per_channel[:, cb : cb + 1])
+            nc.vector.tensor_tensor(window[cb][:].indirect(offsets[:]), scaled[:], beta_wide[cb][:], ADD)
+            nc.sync.dma_start(out_blocks[cb], window[cb][:])

@@ -6,6 +6,7 @@ F, C, S, N = 512, 512, 2048, 512
 FB, CB, JB = F // P, C // P, N // P
 LN_EPS = 1e-5
 FLOPS = 2 * F * C * N
+WARM_UP_MATMULS = 5
 
 BF16, F32, U16 = mybir.dt.bfloat16, mybir.dt.float32, mybir.dt.uint16
 ADD, SUBTRACT, MULT = mybir.AluOpType.add, mybir.AluOpType.subtract, mybir.AluOpType.mult
@@ -17,82 +18,85 @@ def tile_semanticgraphnetwork_kernel(tc, x, w, b, gain, beta, base, offs, out):
     with (
         tc.tile_pool(name="held", bufs=1) as held,
         tc.tile_pool(name="work", bufs=2) as work,
-        tc.tile_pool(name="stat", bufs=4) as stat,
-        tc.psum_pool(name="psum_z", bufs=2) as psum_z,
-        tc.psum_pool(name="psum_t", bufs=2) as psum_t,
-        tc.psum_pool(name="psum_cols", bufs=1) as psum_cols,
+        tc.psum_pool(name="psum_z", bufs=JB) as psum_z,
+        tc.psum_pool(name="psum_t", bufs=3) as psum_t,
+        tc.psum_pool(name="psum_once", bufs=1) as psum_once,
     ):
+        x_sb = held.tile([P, FB, N], BF16, name="x_sb")
+        w_sb = held.tile([P, FB, C], BF16, name="w_sb")
+        x_view = x.rearrange("(fb p) j -> p fb j", p=P)
+        w_view = w.rearrange("(fb p) c -> p fb c", p=P)
+        for half in range(2):
+            blocks = slice(half * FB // 2, (half + 1) * FB // 2)
+            nc.sync.dma_start(x_sb[:, blocks, :], x_view[:, blocks, :])
+            nc.scalar.dma_start(w_sb[:, blocks, :], w_view[:, blocks, :])
+
+        b_rows = held.tile([P, C], F32, name="b_rows")
+        nc.sync.dma_start(b_rows[:], b.rearrange("c one -> (c one)").partition_broadcast(P))
+
         offsets = held.tile([P, N // 16], U16, name="offsets")
         nc.sync.dma_start(offsets[:], offs)
 
-        x_blocks = x.rearrange("(fb p) j -> fb p j", p=P)
-        w_blocks = w.rearrange("(fb p) c -> fb p c", p=P)
-        x_sb = [held.tile([P, N], BF16, name=f"x{fb}") for fb in range(FB)]
-        w_sb = [held.tile([P, C], BF16, name=f"w{fb}") for fb in range(FB)]
-        for fb in range(FB):
-            nc.sync.dma_start(x_sb[fb][:], x_blocks[fb])
-            nc.scalar.dma_start(w_sb[fb][:], w_blocks[fb])
+        gain_cols = held.tile([P, CB], F32, name="gain_cols")
+        beta_cols = held.tile([P, CB], F32, name="beta_cols")
+        nc.scalar.dma_start(gain_cols[:], gain.rearrange("(p cb) one -> p (cb one)", cb=CB))
+        nc.scalar.dma_start(beta_cols[:], beta.rearrange("(p cb) one -> p (cb one)", cb=CB))
 
-        b_rows = held.tile([P, C], F32, name="b_rows")
-        nc.gpsimd.dma_start(b_rows[:], b.rearrange("c one -> (c one)").partition_broadcast(P))
-
-        rows = held.tile([P, P], F32, name="rows")
-        nc.vector.memset(rows[:], 0.0)
-        nc.gpsimd.dma_start(rows[0:CB, :], gain.rearrange("(cb p) one -> cb (p one)", p=P))
-        nc.gpsimd.dma_start(rows[CB : 2 * CB, :], beta.rearrange("(cb p) one -> cb (p one)", p=P))
-
-        base_blocks = base.rearrange("(cb p) s -> cb p s", p=P)
-        out_blocks = out.rearrange("(cb p) s -> cb p s", p=P)
+        base_blocks = base.rearrange("(p cb) s -> cb p s", cb=CB)
+        out_blocks = out.rearrange("(p cb) s -> cb p s", cb=CB)
         window = [held.tile([P, S], F32, name=f"window{cb}") for cb in range(CB)]
         for cb in range(CB):
             queue = nc.sync if cb % 2 == 0 else nc.scalar
             queue.dma_start(window[cb][:], base_blocks[cb])
+
+        cold = held.tile([P, N], BF16, name="cold")
+        nc.vector.memset(cold[:], 0.0)
+        warm_out = psum_once.tile([P, N], F32, name="warm_out")
+        for repeat in range(WARM_UP_MATMULS):
+            nc.tensor.matmul(warm_out[:], cold[:, 0:P], cold[:], start=True, stop=True)
 
         identity = held.tile([P, P], F32, name="identity")
         make_identity(nc, identity[:])
         eps = held.tile([P, 1], F32, name="eps")
         nc.vector.memset(eps[:], LN_EPS)
 
-        rows_flipped = psum_cols.tile([P, P], F32, name="rows_flipped")
-        nc.tensor.transpose(rows_flipped[:], rows[:], identity[:])
-        per_channel = held.tile([P, 2 * CB], F32, name="per_channel")
-        nc.vector.tensor_copy(per_channel[:], rows_flipped[:, 0 : 2 * CB])
-
         zeros = held.tile([P, N], F32, name="zeros")
         nc.gpsimd.memset(zeros[:], 0.0)
         beta_wide = [held.tile([P, N], F32, name=f"beta_wide{cb}") for cb in range(CB)]
         for cb in range(CB):
-            nc.gpsimd.tensor_scalar(beta_wide[cb][:], zeros[:], per_channel[:, CB + cb : CB + cb + 1], None, ADD)
+            nc.gpsimd.tensor_scalar(beta_wide[cb][:], zeros[:], beta_cols[:, cb : cb + 1], None, ADD)
 
+        h = [held.tile([P, C], F32, name=f"h{jb}") for jb in range(JB)]
+        mean_var = [held.tile([P, 2], F32, name=f"mean_var{jb}") for jb in range(JB)]
+        std = [held.tile([P, 1], F32, name=f"std{jb}") for jb in range(JB)]
         normed = [held.tile([P, C], F32, name=f"normed{jb}") for jb in range(JB)]
-        for jb in range(JB):
-            z = psum_z.tile([P, C], F32, name="z")
-            for fb in range(FB):
-                nc.tensor.matmul(
-                    z[:], x_sb[fb][:, jb * P : (jb + 1) * P], w_sb[fb][:], start=(fb == 0), stop=(fb == FB - 1)
-                )
-            biased = work.tile([P, C], F32, name="biased")
-            nc.vector.tensor_tensor(biased[:], z[:], b_rows[:], ADD)
-            h = work.tile([P, C], F32, name="h")
-            nc.scalar.activation(h[:], biased[:], ACT.Relu)
-
-            six = stat.tile([P, 6], F32, name="six")
-            nc.vector.bn_stats(six[:], h[:])
-            mean_var = stat.tile([P, 2], F32, name="mean_var")
-            nc.vector.bn_aggr(mean_var[:], six[:])
-            std = stat.tile([P, 1], F32, name="std")
-            nc.scalar.activation(std[:], mean_var[:, 1:2], ACT.Sqrt, bias=eps[:])
-            rstd = stat.tile([P, 1], F32, name="rstd")
-            nc.vector.reciprocal(rstd[:], std[:])
-            nc.vector.tensor_scalar(normed[jb][:], h[:], mean_var[:, 0:1], rstd[:], SUBTRACT, MULT)
+        for step in range(JB + 1):
+            if step < JB:
+                jb = step
+                z = psum_z.tile([P, C], F32, name="z")
+                for fb in range(FB):
+                    nc.tensor.matmul(
+                        z[:], x_sb[:, fb, jb * P : (jb + 1) * P], w_sb[:, fb, :], start=(fb == 0), stop=(fb == FB - 1)
+                    )
+                biased = work.tile([P, C], F32, name="biased")
+                nc.vector.tensor_tensor(biased[:], z[:], b_rows[:], ADD)
+                nc.vector.tensor_scalar_max(h[jb][:], biased[:], 0.0)
+                six = work.tile([P, 6], F32, name="six")
+                nc.vector.bn_stats(six[:], h[jb][:])
+                nc.vector.bn_aggr(mean_var[jb][:], six[:])
+                nc.scalar.activation(std[jb][:], mean_var[jb][:, 1:2], ACT.Sqrt, bias=eps[:])
+            if step >= 1:
+                jb = step - 1
+                rstd = work.tile([P, 1], F32, name="rstd")
+                nc.vector.reciprocal(rstd[:], std[jb][:])
+                nc.vector.tensor_scalar(normed[jb][:], h[jb][:], mean_var[jb][:, 0:1], rstd[:], SUBTRACT, MULT)
 
         for cb in range(CB):
             flipped = psum_t.tile([P, N], F32, name="flipped")
             for jb in range(JB):
-                nc.tensor.transpose(
-                    flipped[:, jb * P : (jb + 1) * P], normed[jb][:, cb * P : (cb + 1) * P], identity[:]
-                )
+                every_fourth = normed[jb][:].rearrange("j (p cb) -> j cb p", cb=CB)[:, cb, :]
+                nc.tensor.transpose(flipped[:, jb * P : (jb + 1) * P], every_fourth, identity[:])
             scaled = work.tile([P, N], F32, name="scaled")
-            nc.scalar.activation(scaled[:], flipped[:], ACT.Identity, scale=per_channel[:, cb : cb + 1])
+            nc.scalar.activation(scaled[:], flipped[:], ACT.Identity, scale=gain_cols[:, cb : cb + 1])
             nc.vector.tensor_tensor(window[cb][:].indirect(offsets[:]), scaled[:], beta_wide[cb][:], ADD)
             nc.sync.dma_start(out_blocks[cb], window[cb][:])

@@ -68,7 +68,7 @@ def tile_semanticgraphnetwork_kernel(tc, x, w, b, gain, beta, base, offs, out):
 
         h = [held.tile([P, C], F32, name=f"h{jb}") for jb in range(JB)]
         mean_var = [held.tile([P, 2], F32, name=f"mean_var{jb}") for jb in range(JB)]
-        std = [held.tile([P, 1], F32, name=f"std{jb}") for jb in range(JB)]
+        rstd = [held.tile([P, 1], F32, name=f"rstd{jb}") for jb in range(JB)]
         normed = [held.tile([P, C], F32, name=f"normed{jb}") for jb in range(JB)]
         for step in range(JB + 1):
             if step < JB:
@@ -84,12 +84,10 @@ def tile_semanticgraphnetwork_kernel(tc, x, w, b, gain, beta, base, offs, out):
                 six = work.tile([P, 6], F32, name="six")
                 nc.vector.bn_stats(six[:], h[jb][:])
                 nc.vector.bn_aggr(mean_var[jb][:], six[:])
-                nc.scalar.activation(std[jb][:], mean_var[jb][:, 1:2], ACT.Sqrt, bias=eps[:])
+                nc.scalar.activation(rstd[jb][:], mean_var[jb][:, 1:2], ACT.Abs_reciprocal_sqrt, bias=eps[:])
             if step >= 1:
                 jb = step - 1
-                rstd = work.tile([P, 1], F32, name="rstd")
-                nc.vector.reciprocal(rstd[:], std[jb][:])
-                nc.vector.tensor_scalar(normed[jb][:], h[jb][:], mean_var[jb][:, 0:1], rstd[:], SUBTRACT, MULT)
+                nc.vector.tensor_scalar(normed[jb][:], h[jb][:], mean_var[jb][:, 0:1], rstd[jb][:], SUBTRACT, MULT)
 
         for cb in range(CB):
             flipped = psum_t.tile([P, N], F32, name="flipped")
@@ -97,6 +95,9 @@ def tile_semanticgraphnetwork_kernel(tc, x, w, b, gain, beta, base, offs, out):
                 every_fourth = normed[jb][:].rearrange("j (p cb) -> j cb p", cb=CB)[:, cb, :]
                 nc.tensor.transpose(flipped[:, jb * P : (jb + 1) * P], every_fourth, identity[:])
             scaled = work.tile([P, N], F32, name="scaled")
-            nc.scalar.activation(scaled[:], flipped[:], ACT.Identity, scale=gain_cols[:, cb : cb + 1])
+            if cb == 0:
+                nc.vector.tensor_scalar_mul(scaled[:], flipped[:], gain_cols[:, cb : cb + 1])
+            else:
+                nc.scalar.activation(scaled[:], flipped[:], ACT.Identity, scale=gain_cols[:, cb : cb + 1])
             nc.vector.tensor_tensor(window[cb][:].indirect(offsets[:]), scaled[:], beta_wide[cb][:], ADD)
             nc.sync.dma_start(out_blocks[cb], window[cb][:])

@@ -59,6 +59,8 @@ def tile_semanticgraphnetwork_kernel(tc, x, w, b, gain, beta, base, offs, out):
         make_identity(nc, identity[:])
         eps = held.tile([P, 1], F32, name="eps")
         nc.vector.memset(eps[:], LN_EPS)
+        unread = held.tile([P, 1], F32, name="unread")
+        nc.scalar.activation(unread[:], eps[:], ACT.Sqrt)
 
         zeros = held.tile([P, N], F32, name="zeros")
         nc.gpsimd.memset(zeros[:], 0.0)
@@ -67,27 +69,29 @@ def tile_semanticgraphnetwork_kernel(tc, x, w, b, gain, beta, base, offs, out):
             nc.gpsimd.tensor_scalar(beta_wide[cb][:], zeros[:], beta_cols[:, cb : cb + 1], None, ADD)
 
         h = [held.tile([P, C], F32, name=f"h{jb}") for jb in range(JB)]
+        for jb in range(JB):
+            z = psum_z.tile([P, C], F32, name="z")
+            for fb in range(FB):
+                nc.tensor.matmul(
+                    z[:], x_sb[:, fb, jb * P : (jb + 1) * P], w_sb[:, fb, :], start=(fb == 0), stop=(fb == FB - 1)
+                )
+            biased = work.tile([P, C], F32, name="biased")
+            nc.vector.tensor_tensor(biased[:], z[:], b_rows[:], ADD)
+            nc.scalar.activation(h[jb][:], biased[:], ACT.Relu)
+
         mean_var = [held.tile([P, 2], F32, name=f"mean_var{jb}") for jb in range(JB)]
         rstd = [held.tile([P, 1], F32, name=f"rstd{jb}") for jb in range(JB)]
+        for jb in range(JB):
+            six = work.tile([P, 6], F32, name="six")
+            nc.vector.bn_stats(six[:], h[jb][:])
+            nc.vector.bn_aggr(mean_var[jb][:], six[:])
+            std = work.tile([P, 1], F32, name="std")
+            nc.scalar.activation(std[:], mean_var[jb][:, 1:2], ACT.Sqrt, bias=eps[:])
+            nc.vector.reciprocal(rstd[jb][:], std[:])
+
         normed = [held.tile([P, C], F32, name=f"normed{jb}") for jb in range(JB)]
-        for step in range(JB + 1):
-            if step < JB:
-                jb = step
-                z = psum_z.tile([P, C], F32, name="z")
-                for fb in range(FB):
-                    nc.tensor.matmul(
-                        z[:], x_sb[:, fb, jb * P : (jb + 1) * P], w_sb[:, fb, :], start=(fb == 0), stop=(fb == FB - 1)
-                    )
-                biased = work.tile([P, C], F32, name="biased")
-                nc.vector.tensor_tensor(biased[:], z[:], b_rows[:], ADD)
-                nc.vector.tensor_scalar_max(h[jb][:], biased[:], 0.0)
-                six = work.tile([P, 6], F32, name="six")
-                nc.vector.bn_stats(six[:], h[jb][:])
-                nc.vector.bn_aggr(mean_var[jb][:], six[:])
-                nc.scalar.activation(rstd[jb][:], mean_var[jb][:, 1:2], ACT.Abs_reciprocal_sqrt, bias=eps[:])
-            if step >= 1:
-                jb = step - 1
-                nc.vector.tensor_scalar(normed[jb][:], h[jb][:], mean_var[jb][:, 0:1], rstd[jb][:], SUBTRACT, MULT)
+        for jb in range(JB):
+            nc.vector.tensor_scalar(normed[jb][:], h[jb][:], mean_var[jb][:, 0:1], rstd[jb][:], SUBTRACT, MULT)
 
         for cb in range(CB):
             flipped = psum_t.tile([P, N], F32, name="flipped")

@@ -22,6 +22,11 @@ def tile_semanticgraphnetwork_kernel(tc, x, w, b, gain, beta, base, offs, out):
         tc.psum_pool(name="psum_t", bufs=3) as psum_t,
         tc.psum_pool(name="psum_once", bufs=1) as psum_once,
     ):
+        beta_cols = held.tile([P, CB], F32, name="beta_cols")
+        gain_cols = held.tile([P, CB], F32, name="gain_cols")
+        nc.scalar.dma_start(beta_cols[:], beta.rearrange("(p cb) one -> p (cb one)", cb=CB))
+        nc.scalar.dma_start(gain_cols[:], gain.rearrange("(p cb) one -> p (cb one)", cb=CB))
+
         x_sb = held.tile([P, FB, N], BF16, name="x_sb")
         w_sb = held.tile([P, FB, C], BF16, name="w_sb")
         x_view = x.rearrange("(fb p) j -> p fb j", p=P)
@@ -36,11 +41,6 @@ def tile_semanticgraphnetwork_kernel(tc, x, w, b, gain, beta, base, offs, out):
 
         offsets = held.tile([P, N // 16], U16, name="offsets")
         nc.sync.dma_start(offsets[:], offs)
-
-        gain_cols = held.tile([P, CB], F32, name="gain_cols")
-        beta_cols = held.tile([P, CB], F32, name="beta_cols")
-        nc.scalar.dma_start(gain_cols[:], gain.rearrange("(p cb) one -> p (cb one)", cb=CB))
-        nc.scalar.dma_start(beta_cols[:], beta.rearrange("(p cb) one -> p (cb one)", cb=CB))
 
         base_blocks = base.rearrange("(p cb) s -> cb p s", cb=CB)
         out_blocks = out.rearrange("(p cb) s -> cb p s", cb=CB)
@@ -63,10 +63,10 @@ def tile_semanticgraphnetwork_kernel(tc, x, w, b, gain, beta, base, offs, out):
         nc.scalar.activation(unread[:], eps[:], ACT.Sqrt)
 
         zeros = held.tile([P, N], F32, name="zeros")
-        nc.gpsimd.memset(zeros[:], 0.0)
+        nc.vector.memset(zeros[:], 0.0)
         beta_wide = [held.tile([P, N], F32, name=f"beta_wide{cb}") for cb in range(CB)]
         for cb in range(CB):
-            nc.gpsimd.tensor_scalar(beta_wide[cb][:], zeros[:], beta_cols[:, cb : cb + 1], None, ADD)
+            nc.vector.tensor_scalar_add(beta_wide[cb][:], zeros[:], beta_cols[:, cb : cb + 1])
 
         h = [held.tile([P, C], F32, name=f"h{jb}") for jb in range(JB)]
         for jb in range(JB):

@@ -22,11 +22,6 @@ def tile_semanticgraphnetwork_kernel(tc, x, w, b, gain, beta, base, offs, out):
         tc.psum_pool(name="psum_t", bufs=3) as psum_t,
         tc.psum_pool(name="psum_once", bufs=1) as psum_once,
     ):
-        beta_cols = held.tile([P, CB], F32, name="beta_cols")
-        gain_cols = held.tile([P, CB], F32, name="gain_cols")
-        nc.scalar.dma_start(beta_cols[:], beta.rearrange("(p cb) one -> p (cb one)", cb=CB))
-        nc.scalar.dma_start(gain_cols[:], gain.rearrange("(p cb) one -> p (cb one)", cb=CB))
-
         x_sb = held.tile([P, FB, N], BF16, name="x_sb")
         w_sb = held.tile([P, FB, C], BF16, name="w_sb")
         x_view = x.rearrange("(fb p) j -> p fb j", p=P)
@@ -41,6 +36,11 @@ def tile_semanticgraphnetwork_kernel(tc, x, w, b, gain, beta, base, offs, out):
 
         offsets = held.tile([P, N // 16], U16, name="offsets")
         nc.sync.dma_start(offsets[:], offs)
+
+        gain_cols = held.tile([P, CB], F32, name="gain_cols")
+        beta_cols = held.tile([P, CB], F32, name="beta_cols")
+        nc.scalar.dma_start(gain_cols[:], gain.rearrange("(p cb) one -> p (cb one)", cb=CB))
+        nc.scalar.dma_start(beta_cols[:], beta.rearrange("(p cb) one -> p (cb one)", cb=CB))
 
         base_blocks = base.rearrange("(p cb) s -> cb p s", cb=CB)
         out_blocks = out.rearrange("(p cb) s -> cb p s", cb=CB)
@@ -63,10 +63,10 @@ def tile_semanticgraphnetwork_kernel(tc, x, w, b, gain, beta, base, offs, out):
         nc.scalar.activation(unread[:], eps[:], ACT.Sqrt)
 
         zeros = held.tile([P, N], F32, name="zeros")
-        nc.vector.memset(zeros[:], 0.0)
+        nc.gpsimd.memset(zeros[:], 0.0)
         beta_wide = [held.tile([P, N], F32, name=f"beta_wide{cb}") for cb in range(CB)]
         for cb in range(CB):
-            nc.vector.tensor_scalar_add(beta_wide[cb][:], zeros[:], beta_cols[:, cb : cb + 1])
+            nc.gpsimd.tensor_scalar(beta_wide[cb][:], zeros[:], beta_cols[:, cb : cb + 1], None, ADD)
 
         h = [held.tile([P, C], F32, name=f"h{jb}") for jb in range(JB)]
         for jb in range(JB):
@@ -99,9 +99,6 @@ def tile_semanticgraphnetwork_kernel(tc, x, w, b, gain, beta, base, offs, out):
                 every_fourth = normed[jb][:].rearrange("j (p cb) -> j cb p", cb=CB)[:, cb, :]
                 nc.tensor.transpose(flipped[:, jb * P : (jb + 1) * P], every_fourth, identity[:])
             scaled = work.tile([P, N], F32, name="scaled")
-            if cb == 0:
-                nc.vector.tensor_scalar_mul(scaled[:], flipped[:], gain_cols[:, cb : cb + 1])
-            else:
-                nc.scalar.activation(scaled[:], flipped[:], ACT.Identity, scale=gain_cols[:, cb : cb + 1])
+            nc.scalar.activation(scaled[:], flipped[:], ACT.Identity, scale=gain_cols[:, cb : cb + 1])
             nc.vector.tensor_tensor(window[cb][:].indirect(offsets[:]), scaled[:], beta_wide[cb][:], ADD)
             nc.sync.dma_start(out_blocks[cb], window[cb][:])

@@ -9,7 +9,7 @@ FLOPS = 2 * F * C * N
 WARM_UP_MATMULS = 5
 
 BF16, F32, U16 = mybir.dt.bfloat16, mybir.dt.float32, mybir.dt.uint16
-ADD, SUBTRACT, MULT = mybir.AluOpType.add, mybir.AluOpType.subtract, mybir.AluOpType.mult
+ADD, MULT = mybir.AluOpType.add, mybir.AluOpType.mult
 ACT = mybir.ActivationFunctionType
 
 
@@ -69,6 +69,7 @@ def tile_semanticgraphnetwork_kernel(tc, x, w, b, gain, beta, base, offs, out):
             nc.gpsimd.tensor_scalar(beta_wide[cb][:], zeros[:], beta_cols[:, cb : cb + 1], None, ADD)
 
         h = [held.tile([P, C], F32, name=f"h{jb}") for jb in range(JB)]
+        sum_h = [held.tile([P, 1], F32, name=f"sum_h{jb}") for jb in range(JB)]
         for jb in range(JB):
             z = psum_z.tile([P, C], F32, name="z")
             for fb in range(FB):
@@ -77,21 +78,22 @@ def tile_semanticgraphnetwork_kernel(tc, x, w, b, gain, beta, base, offs, out):
                 )
             biased = work.tile([P, C], F32, name="biased")
             nc.vector.tensor_tensor(biased[:], z[:], b_rows[:], ADD)
-            nc.scalar.activation(h[jb][:], biased[:], ACT.Relu)
+            nc.scalar.activation(h[jb][:], biased[:], ACT.Relu, accum_out=sum_h[jb][:])
 
-        mean_var = [held.tile([P, 2], F32, name=f"mean_var{jb}") for jb in range(JB)]
+        neg_mean = [held.tile([P, 1], F32, name=f"neg_mean{jb}") for jb in range(JB)]
         rstd = [held.tile([P, 1], F32, name=f"rstd{jb}") for jb in range(JB)]
         for jb in range(JB):
-            six = work.tile([P, 6], F32, name="six")
-            nc.vector.bn_stats(six[:], h[jb][:])
-            nc.vector.bn_aggr(mean_var[jb][:], six[:])
+            nc.scalar.mul(neg_mean[jb][:], sum_h[jb][:], -1.0 / C)
+            squares = work.tile([P, C], F32, name="squares")
+            sum_squares = work.tile([P, 1], F32, name="sum_squares")
+            nc.scalar.activation(squares[:], h[jb][:], ACT.Square, bias=neg_mean[jb][:], accum_out=sum_squares[:])
             std = work.tile([P, 1], F32, name="std")
-            nc.scalar.activation(std[:], mean_var[jb][:, 1:2], ACT.Sqrt, bias=eps[:])
+            nc.scalar.activation(std[:], sum_squares[:], ACT.Sqrt, bias=eps[:], scale=1.0 / C)
             nc.vector.reciprocal(rstd[jb][:], std[:])
 
         normed = [held.tile([P, C], F32, name=f"normed{jb}") for jb in range(JB)]
         for jb in range(JB):
-            nc.vector.tensor_scalar(normed[jb][:], h[jb][:], mean_var[jb][:, 0:1], rstd[jb][:], SUBTRACT, MULT)
+            nc.vector.tensor_scalar(normed[jb][:], h[jb][:], neg_mean[jb][:], rstd[jb][:], ADD, MULT)
 
         for cb in range(CB):
             flipped = psum_t.tile([P, N], F32, name="flipped")

@@ -9,7 +9,7 @@ FLOPS = 2 * F * C * N
 WARM_UP_MATMULS = 5
 
 BF16, F32, U16 = mybir.dt.bfloat16, mybir.dt.float32, mybir.dt.uint16
-ADD, MULT = mybir.AluOpType.add, mybir.AluOpType.mult
+ADD, SUBTRACT, MULT = mybir.AluOpType.add, mybir.AluOpType.subtract, mybir.AluOpType.mult
 ACT = mybir.ActivationFunctionType
 
 
@@ -66,10 +66,9 @@ def tile_semanticgraphnetwork_kernel(tc, x, w, b, gain, beta, base, offs, out):
         nc.gpsimd.memset(zeros[:], 0.0)
         beta_wide = [held.tile([P, N], F32, name=f"beta_wide{cb}") for cb in range(CB)]
         for cb in range(CB):
-            nc.gpsimd.tensor_scalar(beta_wide[cb][:], zeros[:], beta_cols[:, cb : cb + 1], None, ADD)
+            nc.gpsimd.tensor_scalar(beta_wide[cb][:], zeros[:], 1.0, beta_cols[:, cb : cb + 1], MULT, ADD)
 
         h = [held.tile([P, C], F32, name=f"h{jb}") for jb in range(JB)]
-        sum_h = [held.tile([P, 1], F32, name=f"sum_h{jb}") for jb in range(JB)]
         for jb in range(JB):
             z = psum_z.tile([P, C], F32, name="z")
             for fb in range(FB):
@@ -78,22 +77,21 @@ def tile_semanticgraphnetwork_kernel(tc, x, w, b, gain, beta, base, offs, out):
                 )
             biased = work.tile([P, C], F32, name="biased")
             nc.vector.tensor_tensor(biased[:], z[:], b_rows[:], ADD)
-            nc.scalar.activation(h[jb][:], biased[:], ACT.Relu, accum_out=sum_h[jb][:])
+            nc.scalar.activation(h[jb][:], biased[:], ACT.Relu)
 
-        neg_mean = [held.tile([P, 1], F32, name=f"neg_mean{jb}") for jb in range(JB)]
+        mean_var = [held.tile([P, 2], F32, name=f"mean_var{jb}") for jb in range(JB)]
         rstd = [held.tile([P, 1], F32, name=f"rstd{jb}") for jb in range(JB)]
         for jb in range(JB):
-            nc.scalar.mul(neg_mean[jb][:], sum_h[jb][:], -1.0 / C)
-            squares = work.tile([P, C], F32, name="squares")
-            sum_squares = work.tile([P, 1], F32, name="sum_squares")
-            nc.scalar.activation(squares[:], h[jb][:], ACT.Square, bias=neg_mean[jb][:], accum_out=sum_squares[:])
+            six = work.tile([P, 6], F32, name="six")
+            nc.vector.bn_stats(six[:], h[jb][:])
+            nc.vector.bn_aggr(mean_var[jb][:], six[:])
             std = work.tile([P, 1], F32, name="std")
-            nc.scalar.activation(std[:], sum_squares[:], ACT.Sqrt, bias=eps[:], scale=1.0 / C)
+            nc.scalar.activation(std[:], mean_var[jb][:, 1:2], ACT.Sqrt, bias=eps[:])
             nc.vector.reciprocal(rstd[jb][:], std[:])
 
         normed = [held.tile([P, C], F32, name=f"normed{jb}") for jb in range(JB)]
         for jb in range(JB):
-            nc.vector.tensor_scalar(normed[jb][:], h[jb][:], neg_mean[jb][:], rstd[jb][:], ADD, MULT)
+            nc.vector.tensor_scalar(normed[jb][:], h[jb][:], mean_var[jb][:, 0:1], rstd[jb][:], SUBTRACT, MULT)
 
         for cb in range(CB):
             flipped = psum_t.tile([P, N], F32, name="flipped")

@@ -18,6 +18,7 @@ def tile_semanticgraphnetwork_kernel(tc, x, w, b, gain, beta, base, offs, out):
     with (
         tc.tile_pool(name="held", bufs=1) as held,
         tc.tile_pool(name="work", bufs=2) as work,
+        tc.tile_pool(name="squares", bufs=4) as squares,
         tc.psum_pool(name="psum_z", bufs=JB) as psum_z,
         tc.psum_pool(name="psum_t", bufs=3) as psum_t,
         tc.psum_pool(name="psum_once", bufs=1) as psum_once,
@@ -39,11 +40,11 @@ def tile_semanticgraphnetwork_kernel(tc, x, w, b, gain, beta, base, offs, out):
 
         gain_cols = held.tile([P, CB], F32, name="gain_cols")
         beta_cols = held.tile([P, CB], F32, name="beta_cols")
-        nc.scalar.dma_start(gain_cols[:], gain.rearrange("(p cb) one -> p (cb one)", cb=CB))
-        nc.scalar.dma_start(beta_cols[:], beta.rearrange("(p cb) one -> p (cb one)", cb=CB))
+        nc.scalar.dma_start(gain_cols[:], gain.rearrange("(cb p) one -> p (cb one)", p=P))
+        nc.scalar.dma_start(beta_cols[:], beta.rearrange("(cb p) one -> p (cb one)", p=P))
 
-        base_blocks = base.rearrange("(p cb) s -> cb p s", cb=CB)
-        out_blocks = out.rearrange("(p cb) s -> cb p s", cb=CB)
+        base_blocks = base.rearrange("(cb p) s -> cb p s", p=P)
+        out_blocks = out.rearrange("(cb p) s -> cb p s", p=P)
         window = [held.tile([P, S], F32, name=f"window{cb}") for cb in range(CB)]
         for cb in range(CB):
             queue = nc.sync if cb % 2 == 0 else nc.scalar
@@ -60,7 +61,7 @@ def tile_semanticgraphnetwork_kernel(tc, x, w, b, gain, beta, base, offs, out):
         eps = held.tile([P, 1], F32, name="eps")
         nc.vector.memset(eps[:], LN_EPS)
         unread = held.tile([P, 1], F32, name="unread")
-        nc.scalar.activation(unread[:], eps[:], ACT.Sqrt)
+        nc.scalar.activation(unread[:], eps[:], ACT.Abs_reciprocal_sqrt)
 
         zeros = held.tile([P, N], F32, name="zeros")
         nc.gpsimd.memset(zeros[:], 0.0)
@@ -81,24 +82,31 @@ def tile_semanticgraphnetwork_kernel(tc, x, w, b, gain, beta, base, offs, out):
 
         mean_var = [held.tile([P, 2], F32, name=f"mean_var{jb}") for jb in range(JB)]
         rstd = [held.tile([P, 1], F32, name=f"rstd{jb}") for jb in range(JB)]
+        shift = [held.tile([P, 1], F32, name=f"shift{jb}") for jb in range(JB)]
         for jb in range(JB):
             six = work.tile([P, 6], F32, name="six")
             nc.vector.bn_stats(six[:], h[jb][:])
             nc.vector.bn_aggr(mean_var[jb][:], six[:])
-            std = work.tile([P, 1], F32, name="std")
-            nc.scalar.activation(std[:], mean_var[jb][:, 1:2], ACT.Sqrt, bias=eps[:])
-            nc.vector.reciprocal(rstd[jb][:], std[:])
-
-        normed = [held.tile([P, C], F32, name=f"normed{jb}") for jb in range(JB)]
-        for jb in range(JB):
-            nc.vector.tensor_scalar(normed[jb][:], h[jb][:], mean_var[jb][:, 0:1], rstd[jb][:], SUBTRACT, MULT)
+            nc.scalar.activation(rstd[jb][:], mean_var[jb][:, 1:2], ACT.Abs_reciprocal_sqrt, bias=eps[:])
+            nc.vector.tensor_scalar(shift[jb][:], mean_var[jb][:, 0:1], rstd[jb][:], -1.0, MULT, MULT)
 
         for cb in range(CB):
-            flipped = psum_t.tile([P, N], F32, name="flipped")
-            for jb in range(JB):
-                every_fourth = normed[jb][:].rearrange("j (p cb) -> j cb p", cb=CB)[:, cb, :]
-                nc.tensor.transpose(flipped[:, jb * P : (jb + 1) * P], every_fourth, identity[:])
+            channels = slice(cb * P, (cb + 1) * P)
             scaled = work.tile([P, N], F32, name="scaled")
-            nc.scalar.activation(scaled[:], flipped[:], ACT.Identity, scale=gain_cols[:, cb : cb + 1])
+            for jb in range(JB):
+                normed = squares.tile([P, P], F32, name="normed")
+                if cb == 0:
+                    nc.vector.tensor_scalar(
+                        normed[:], h[jb][:, channels], mean_var[jb][:, 0:1], rstd[jb][:], SUBTRACT, MULT
+                    )
+                else:
+                    nc.scalar.activation(
+                        normed[:], h[jb][:, channels], ACT.Identity, bias=shift[jb][:], scale=rstd[jb][:]
+                    )
+                flipped = psum_t.tile([P, P], F32, name="flipped")
+                nc.tensor.transpose(flipped[:], normed[:], identity[:])
+                nc.scalar.activation(
+                    scaled[:, jb * P : (jb + 1) * P], flipped[:], ACT.Identity, scale=gain_cols[:, cb : cb + 1]
+                )
             nc.vector.tensor_tensor(window[cb][:].indirect(offsets[:]), scaled[:], beta_wide[cb][:], ADD)
             nc.sync.dma_start(out_blocks[cb], window[cb][:])

@@ -18,7 +18,7 @@ def tile_semanticgraphnetwork_kernel(tc, x, w, b, gain, beta, base, offs, out):
     with (
         tc.tile_pool(name="held", bufs=1) as held,
         tc.tile_pool(name="work", bufs=2) as work,
-        tc.tile_pool(name="squares", bufs=4) as squares,
+        tc.tile_pool(name="squares", bufs=2) as squares,
         tc.psum_pool(name="psum_z", bufs=JB) as psum_z,
         tc.psum_pool(name="psum_t", bufs=3) as psum_t,
         tc.psum_pool(name="psum_once", bufs=1) as psum_once,
@@ -69,44 +69,64 @@ def tile_semanticgraphnetwork_kernel(tc, x, w, b, gain, beta, base, offs, out):
         for cb in range(CB):
             nc.gpsimd.tensor_scalar(beta_wide[cb][:], zeros[:], 1.0, beta_cols[:, cb : cb + 1], MULT, ADD)
 
-        h = [held.tile([P, C], F32, name=f"h{jb}") for jb in range(JB)]
+        z = []
         for jb in range(JB):
-            z = psum_z.tile([P, C], F32, name="z")
+            z.append(psum_z.tile([P, C], F32, name="z"))
             for fb in range(FB):
                 nc.tensor.matmul(
-                    z[:], x_sb[:, fb, jb * P : (jb + 1) * P], w_sb[:, fb, :], start=(fb == 0), stop=(fb == FB - 1)
+                    z[jb][:], x_sb[:, fb, jb * P : (jb + 1) * P], w_sb[:, fb, :], start=(fb == 0), stop=(fb == FB - 1)
                 )
-            biased = work.tile([P, C], F32, name="biased")
-            nc.vector.tensor_tensor(biased[:], z[:], b_rows[:], ADD)
-            nc.scalar.activation(h[jb][:], biased[:], ACT.Relu)
 
+        h = [held.tile([P, C], F32, name=f"h{jb}") for jb in range(JB)]
         mean_var = [held.tile([P, 2], F32, name=f"mean_var{jb}") for jb in range(JB)]
         rstd = [held.tile([P, 1], F32, name=f"rstd{jb}") for jb in range(JB)]
+        for on_vector in range(0, JB, 2):
+            on_scalar = on_vector + 1
+            h_sum = work.tile([P, 1], F32, name="h_sum")
+            for jb in (on_vector, on_scalar):
+                biased = work.tile([P, C], F32, name="biased")
+                nc.vector.tensor_tensor(biased[:], z[jb][:], b_rows[:], ADD)
+                if jb == on_scalar:
+                    nc.scalar.activation(h[jb][:], biased[:], ACT.Relu, accum_out=h_sum[:])
+                else:
+                    nc.scalar.activation(h[jb][:], biased[:], ACT.Relu)
+
+            unread_squares = work.tile([P, C], F32, name="unread_squares")
+            square_sum = work.tile([P, 1], F32, name="square_sum")
+            nc.scalar.activation(
+                unread_squares[:], h[on_scalar][:], ACT.Square, bias=h_sum[:], scale=-float(C), accum_out=square_sum[:]
+            )
+            six = work.tile([P, 6], F32, name="six")
+            nc.vector.bn_stats(six[:], h[on_vector][:])
+            nc.vector.bn_aggr(mean_var[on_vector][:], six[:])
+            nc.vector.tensor_scalar(mean_var[on_scalar][:, 0:1], h_sum[:], 1.0 / C, None, MULT)
+
+            nc.scalar.activation(rstd[on_vector][:], mean_var[on_vector][:, 1:2], ACT.Abs_reciprocal_sqrt, bias=eps[:])
+            nc.scalar.activation(rstd[on_scalar][:], square_sum[:], ACT.Abs_reciprocal_sqrt, bias=eps[:], scale=1.0 / C**3)
+
+        def normalised_squares():
+            return [squares.tile([P, P], F32, name=f"normed{jb}") for jb in range(JB)]
+
+        normed = normalised_squares()
+        for jb in range(JB):
+            nc.vector.tensor_scalar(normed[jb][:], h[jb][:, 0:P], mean_var[jb][:, 0:1], rstd[jb][:], SUBTRACT, MULT)
         shift = [held.tile([P, 1], F32, name=f"shift{jb}") for jb in range(JB)]
         for jb in range(JB):
-            six = work.tile([P, 6], F32, name="six")
-            nc.vector.bn_stats(six[:], h[jb][:])
-            nc.vector.bn_aggr(mean_var[jb][:], six[:])
-            nc.scalar.activation(rstd[jb][:], mean_var[jb][:, 1:2], ACT.Abs_reciprocal_sqrt, bias=eps[:])
             nc.vector.tensor_scalar(shift[jb][:], mean_var[jb][:, 0:1], rstd[jb][:], -1.0, MULT, MULT)
 
         for cb in range(CB):
-            channels = slice(cb * P, (cb + 1) * P)
             scaled = work.tile([P, N], F32, name="scaled")
             for jb in range(JB):
-                normed = squares.tile([P, P], F32, name="normed")
-                if cb == 0:
-                    nc.vector.tensor_scalar(
-                        normed[:], h[jb][:, channels], mean_var[jb][:, 0:1], rstd[jb][:], SUBTRACT, MULT
-                    )
-                else:
-                    nc.scalar.activation(
-                        normed[:], h[jb][:, channels], ACT.Identity, bias=shift[jb][:], scale=rstd[jb][:]
-                    )
                 flipped = psum_t.tile([P, P], F32, name="flipped")
-                nc.tensor.transpose(flipped[:], normed[:], identity[:])
+                nc.tensor.transpose(flipped[:], normed[jb][:], identity[:])
                 nc.scalar.activation(
                     scaled[:, jb * P : (jb + 1) * P], flipped[:], ACT.Identity, scale=gain_cols[:, cb : cb + 1]
                 )
+            if cb + 1 < CB:
+                normed = normalised_squares()
+                for jb in range(JB):
+                    nc.scalar.activation(
+                        normed[jb][:], h[jb][:, (cb + 1) * P : (cb + 2) * P], ACT.Identity, bias=shift[jb][:], scale=rstd[jb][:]
+                    )
             nc.vector.tensor_tensor(window[cb][:].indirect(offsets[:]), scaled[:], beta_wide[cb][:], ADD)
             nc.sync.dma_start(out_blocks[cb], window[cb][:])

@@ -18,7 +18,6 @@ def tile_semanticgraphnetwork_kernel(tc, x, w, b, gain, beta, base, offs, out):
     with (
         tc.tile_pool(name="held", bufs=1) as held,
         tc.tile_pool(name="work", bufs=2) as work,
-        tc.tile_pool(name="squares", bufs=2) as squares,
         tc.psum_pool(name="psum_z", bufs=JB) as psum_z,
         tc.psum_pool(name="psum_t", bufs=3) as psum_t,
         tc.psum_pool(name="psum_once", bufs=1) as psum_once,
@@ -104,29 +103,27 @@ def tile_semanticgraphnetwork_kernel(tc, x, w, b, gain, beta, base, offs, out):
             nc.scalar.activation(rstd[on_vector][:], mean_var[on_vector][:, 1:2], ACT.Abs_reciprocal_sqrt, bias=eps[:])
             nc.scalar.activation(rstd[on_scalar][:], square_sum[:], ACT.Abs_reciprocal_sqrt, bias=eps[:], scale=1.0 / C**3)
 
-        def normalised_squares():
-            return [squares.tile([P, P], F32, name=f"normed{jb}") for jb in range(JB)]
-
-        normed = normalised_squares()
-        for jb in range(JB):
-            nc.vector.tensor_scalar(normed[jb][:], h[jb][:, 0:P], mean_var[jb][:, 0:1], rstd[jb][:], SUBTRACT, MULT)
-        shift = [held.tile([P, 1], F32, name=f"shift{jb}") for jb in range(JB)]
-        for jb in range(JB):
-            nc.vector.tensor_scalar(shift[jb][:], mean_var[jb][:, 0:1], rstd[jb][:], -1.0, MULT, MULT)
+        normed = [held.tile([P, C], F32, name=f"normed{jb}") for jb in range(JB)]
+        for node_blocks, pieces in (((0, 1), (slice(0, C),)), ((2, 3), (slice(0, P), slice(P, C)))):
+            for channels in pieces:
+                for jb in node_blocks:
+                    nc.vector.tensor_scalar(
+                        normed[jb][:, channels], h[jb][:, channels], mean_var[jb][:, 0:1], rstd[jb][:], SUBTRACT, MULT
+                    )
 
         for cb in range(CB):
             scaled = work.tile([P, N], F32, name="scaled")
-            for jb in range(JB):
-                flipped = psum_t.tile([P, P], F32, name="flipped")
-                nc.tensor.transpose(flipped[:], normed[jb][:], identity[:])
-                nc.scalar.activation(
-                    scaled[:, jb * P : (jb + 1) * P], flipped[:], ACT.Identity, scale=gain_cols[:, cb : cb + 1]
-                )
-            if cb + 1 < CB:
-                normed = normalised_squares()
+            if cb == 0:
                 for jb in range(JB):
+                    square = psum_t.tile([P, P], F32, name="square", tag="bank")
+                    nc.tensor.transpose(square[:], normed[jb][:, 0:P], identity[:])
                     nc.scalar.activation(
-                        normed[jb][:], h[jb][:, (cb + 1) * P : (cb + 2) * P], ACT.Identity, bias=shift[jb][:], scale=rstd[jb][:]
+                        scaled[:, jb * P : (jb + 1) * P], square[:], ACT.Identity, scale=gain_cols[:, 0:1]
                     )
+            else:
+                flipped = psum_t.tile([P, N], F32, name="flipped", tag="bank")
+                for jb in range(JB):
+                    nc.tensor.transpose(flipped[:, jb * P : (jb + 1) * P], normed[jb][:, cb * P : (cb + 1) * P], identity[:])
+                nc.scalar.activation(scaled[:], flipped[:], ACT.Identity, scale=gain_cols[:, cb : cb + 1])
             nc.vector.tensor_tensor(window[cb][:].indirect(offsets[:]), scaled[:], beta_wide[cb][:], ADD)
             nc.sync.dma_start(out_blocks[cb], window[cb][:])

@@ -39,8 +39,8 @@ def tile_semanticgraphnetwork_kernel(tc, x, w, b, gain, beta, base, offs, out):
 
         gain_cols = held.tile([P, CB], F32, name="gain_cols")
         beta_cols = held.tile([P, CB], F32, name="beta_cols")
-        nc.scalar.dma_start(gain_cols[:], gain.rearrange("(cb p) one -> p (cb one)", p=P))
         nc.scalar.dma_start(beta_cols[:], beta.rearrange("(cb p) one -> p (cb one)", p=P))
+        nc.scalar.dma_start(gain_cols[:], gain.rearrange("(cb p) one -> p (cb one)", p=P))
 
         base_blocks = base.rearrange("(cb p) s -> cb p s", p=P)
         out_blocks = out.rearrange("(cb p) s -> cb p s", p=P)

@@ -39,11 +39,11 @@ def tile_semanticgraphnetwork_kernel(tc, x, w, b, gain, beta, base, offs, out):
 
         gain_cols = held.tile([P, CB], F32, name="gain_cols")
         beta_cols = held.tile([P, CB], F32, name="beta_cols")
-        nc.scalar.dma_start(beta_cols[:], beta.rearrange("(cb p) one -> p (cb one)", p=P))
-        nc.scalar.dma_start(gain_cols[:], gain.rearrange("(cb p) one -> p (cb one)", p=P))
+        nc.scalar.dma_start(beta_cols[:], beta.rearrange("(p cb) one -> p (cb one)", cb=CB))
+        nc.scalar.dma_start(gain_cols[:], gain.rearrange("(p cb) one -> p (cb one)", cb=CB))
 
-        base_blocks = base.rearrange("(cb p) s -> cb p s", p=P)
-        out_blocks = out.rearrange("(cb p) s -> cb p s", p=P)
+        base_blocks = base.rearrange("(p cb) s -> cb p s", cb=CB)
+        out_blocks = out.rearrange("(p cb) s -> cb p s", cb=CB)
         window = [held.tile([P, S], F32, name=f"window{cb}") for cb in range(CB)]
         for cb in range(CB):
             queue = nc.sync if cb % 2 == 0 else nc.scalar
@@ -104,26 +104,25 @@ def tile_semanticgraphnetwork_kernel(tc, x, w, b, gain, beta, base, offs, out):
             nc.scalar.activation(rstd[on_scalar][:], square_sum[:], ACT.Abs_reciprocal_sqrt, bias=eps[:], scale=1.0 / C**3)
 
         normed = [held.tile([P, C], F32, name=f"normed{jb}") for jb in range(JB)]
-        for node_blocks, pieces in (((0, 1), (slice(0, C),)), ((2, 3), (slice(0, P), slice(P, C)))):
-            for channels in pieces:
-                for jb in node_blocks:
-                    nc.vector.tensor_scalar(
-                        normed[jb][:, channels], h[jb][:, channels], mean_var[jb][:, 0:1], rstd[jb][:], SUBTRACT, MULT
-                    )
+        for jb in range(JB):
+            nc.vector.tensor_scalar(normed[jb][:], h[jb][:], mean_var[jb][:, 0:1], rstd[jb][:], SUBTRACT, MULT)
+
+        def channel_block(jb, cb):
+            return normed[jb][:].rearrange("j (p cb) -> j cb p", cb=CB)[:, cb, :]
 
         for cb in range(CB):
             scaled = work.tile([P, N], F32, name="scaled")
             if cb == 0:
                 for jb in range(JB):
                     square = psum_t.tile([P, P], F32, name="square", tag="bank")
-                    nc.tensor.transpose(square[:], normed[jb][:, 0:P], identity[:])
+                    nc.tensor.transpose(square[:], channel_block(jb, 0), identity[:])
                     nc.scalar.activation(
                         scaled[:, jb * P : (jb + 1) * P], square[:], ACT.Identity, scale=gain_cols[:, 0:1]
                     )
             else:
                 flipped = psum_t.tile([P, N], F32, name="flipped", tag="bank")
                 for jb in range(JB):
-                    nc.tensor.transpose(flipped[:, jb * P : (jb + 1) * P], normed[jb][:, cb * P : (cb + 1) * P], identity[:])
+                    nc.tensor.transpose(flipped[:, jb * P : (jb + 1) * P], channel_block(jb, cb), identity[:])
                 nc.scalar.activation(scaled[:], flipped[:], ACT.Identity, scale=gain_cols[:, cb : cb + 1])
             nc.vector.tensor_tensor(window[cb][:].indirect(offsets[:]), scaled[:], beta_wide[cb][:], ADD)
             nc.sync.dma_start(out_blocks[cb], window[cb][:])

@@ -6,7 +6,7 @@ F, C, S, N = 512, 512, 2048, 512
 FB, CB, JB = F // P, C // P, N // P
 LN_EPS = 1e-5
 FLOPS = 2 * F * C * N
-WARM_UP_MATMULS = 5
+WARM_UP_MATMULS = 3
 
 BF16, F32, U16 = mybir.dt.bfloat16, mybir.dt.float32, mybir.dt.uint16
 ADD, SUBTRACT, MULT = mybir.AluOpType.add, mybir.AluOpType.subtract, mybir.AluOpType.mult

@@ -24,8 +24,8 @@ def tile_semanticgraphnetwork_kernel(tc, x, w, b, gain, beta, base, offs, out):
     ):
         x_sb = held.tile([P, FB, N], BF16, name="x_sb")
         w_sb = held.tile([P, FB, C], BF16, name="w_sb")
-        x_view = x.rearrange("(fb p) j -> p fb j", p=P)
-        w_view = w.rearrange("(fb p) c -> p fb c", p=P)
+        x_view = x.rearrange("(p fb) j -> p fb j", fb=FB)
+        w_view = w.rearrange("(p fb) c -> p fb c", fb=FB)
         for half in range(2):
             blocks = slice(half * FB // 2, (half + 1) * FB // 2)
             nc.sync.dma_start(x_sb[:, blocks, :], x_view[:, blocks, :])

@@ -31,6 +31,11 @@ def tile_semanticgraphnetwork_kernel(tc, x, w, b, gain, beta, base, offs, out):
             nc.sync.dma_start(x_sb[:, blocks, :], x_view[:, blocks, :])
             nc.scalar.dma_start(w_sb[:, blocks, :], w_view[:, blocks, :])
 
+        eps = held.tile([P, 1], F32, name="eps")
+        nc.vector.memset(eps[:], LN_EPS)
+        unread = held.tile([P, 1], F32, name="unread")
+        nc.scalar.activation(unread[:], eps[:], ACT.Abs_reciprocal_sqrt)
+
         b_rows = held.tile([P, C], F32, name="b_rows")
         nc.sync.dma_start(b_rows[:], b.rearrange("c one -> (c one)").partition_broadcast(P))
 
@@ -46,8 +51,7 @@ def tile_semanticgraphnetwork_kernel(tc, x, w, b, gain, beta, base, offs, out):
         out_blocks = out.rearrange("(p cb) s -> cb p s", cb=CB)
         window = [held.tile([P, S], F32, name=f"window{cb}") for cb in range(CB)]
         for cb in range(CB):
-            queue = nc.sync if cb % 2 == 0 else nc.scalar
-            queue.dma_start(window[cb][:], base_blocks[cb])
+            nc.sync.dma_start(window[cb][:], base_blocks[cb])
 
         cold = held.tile([P, N], BF16, name="cold")
         nc.vector.memset(cold[:], 0.0)
@@ -57,10 +61,6 @@ def tile_semanticgraphnetwork_kernel(tc, x, w, b, gain, beta, base, offs, out):
 
         identity = held.tile([P, P], F32, name="identity")
         make_identity(nc, identity[:])
-        eps = held.tile([P, 1], F32, name="eps")
-        nc.vector.memset(eps[:], LN_EPS)
-        unread = held.tile([P, 1], F32, name="unread")
-        nc.scalar.activation(unread[:], eps[:], ACT.Abs_reciprocal_sqrt)
 
         zeros = held.tile([P, N], F32, name="zeros")
         nc.gpsimd.memset(zeros[:], 0.0)

@@ -5,6 +5,8 @@ P = 128
 F, C, S, N = 512, 512, 2048, 512
 FB, CB, JB = F // P, C // P, N // P
 LN_EPS = 1e-5
+B_TERMS = 3
+B_ROWS = 4
 FLOPS = 2 * F * C * N
 WARM_UP_MATMULS = 3
 
@@ -22,6 +24,8 @@ def tile_semanticgraphnetwork_kernel(tc, x, w, b, gain, beta, base, offs, out):
         tc.psum_pool(name="psum_t", bufs=3) as psum_t,
         tc.psum_pool(name="psum_once", bufs=1) as psum_once,
     ):
+        b_rows = held.tile([B_ROWS, C], F32, name="b_rows")
+        nc.sync.dma_start(b_rows[:], b.rearrange("c one -> (c one)").partition_broadcast(B_ROWS))
         x_sb = held.tile([P, FB, N], BF16, name="x_sb")
         w_sb = held.tile([P, FB, C], BF16, name="w_sb")
         x_view = x.rearrange("(p fb) j -> p fb j", fb=FB)
@@ -35,9 +39,6 @@ def tile_semanticgraphnetwork_kernel(tc, x, w, b, gain, beta, base, offs, out):
         nc.vector.memset(eps[:], LN_EPS)
         unread = held.tile([P, 1], F32, name="unread")
         nc.scalar.activation(unread[:], eps[:], ACT.Abs_reciprocal_sqrt)
-
-        b_rows = held.tile([P, C], F32, name="b_rows")
-        nc.sync.dma_start(b_rows[:], b.rearrange("c one -> (c one)").partition_broadcast(P))
 
         offsets = held.tile([P, N // 16], U16, name="offsets")
         nc.sync.dma_start(offsets[:], offs)
@@ -62,6 +63,24 @@ def tile_semanticgraphnetwork_kernel(tc, x, w, b, gain, beta, base, offs, out):
         identity = held.tile([P, P], F32, name="identity")
         make_identity(nc, identity[:])
 
+        minus_identity = held.tile([B_ROWS, B_ROWS], F32, name="minus_identity")
+        nc.vector.tensor_scalar(minus_identity[:], identity[0:B_ROWS, 0:B_ROWS], -1.0, None, MULT)
+        minus_from_row_1 = held.tile([B_ROWS, 1], F32, name="minus_from_row_1")
+        nc.vector.tensor_scalar(minus_from_row_1[:], identity[0:B_ROWS, 0:1], 1.0, None, SUBTRACT)
+        minus_in_row_2 = minus_identity[:, 2:3]
+        ones = held.tile([P, P], BF16, name="ones")
+        nc.vector.memset(ones[:], 0.0)
+        nc.vector.memset(ones[0:B_TERMS, :], 1.0)
+        b_terms = held.tile([P, C], BF16, name="b_terms")
+        nc.vector.memset(b_terms[:], 0.0)
+        first = held.tile([B_ROWS, C], BF16, name="first")
+        nc.vector.tensor_copy(first[:], b_rows[:])
+        rest = held.tile([B_ROWS, C], F32, name="rest")
+        nc.vector.scalar_tensor_tensor(rest[:], first[:], minus_from_row_1[:], b_rows[:], MULT, ADD)
+        second = held.tile([B_ROWS, C], BF16, name="second")
+        nc.vector.tensor_copy(second[:], rest[:])
+        nc.vector.scalar_tensor_tensor(b_terms[0:B_ROWS, :], second[:], minus_in_row_2, rest[:], MULT, ADD)
+
         zeros = held.tile([P, N], F32, name="zeros")
         nc.gpsimd.memset(zeros[:], 0.0)
         beta_wide = [held.tile([P, N], F32, name=f"beta_wide{cb}") for cb in range(CB)]
@@ -73,8 +92,9 @@ def tile_semanticgraphnetwork_kernel(tc, x, w, b, gain, beta, base, offs, out):
             z.append(psum_z.tile([P, C], F32, name="z"))
             for fb in range(FB):
                 nc.tensor.matmul(
-                    z[jb][:], x_sb[:, fb, jb * P : (jb + 1) * P], w_sb[:, fb, :], start=(fb == 0), stop=(fb == FB - 1)
+                    z[jb][:], x_sb[:, fb, jb * P : (jb + 1) * P], w_sb[:, fb, :], start=(fb == 0), stop=False
                 )
+            nc.tensor.matmul(z[jb][:], ones[:], b_terms[:], start=False, stop=True)
 
         h = [held.tile([P, C], F32, name=f"h{jb}") for jb in range(JB)]
         mean_var = [held.tile([P, 2], F32, name=f"mean_var{jb}") for jb in range(JB)]
@@ -83,12 +103,10 @@ def tile_semanticgraphnetwork_kernel(tc, x, w, b, gain, beta, base, offs, out):
             on_scalar = on_vector + 1
             h_sum = work.tile([P, 1], F32, name="h_sum")
             for jb in (on_vector, on_scalar):
-                biased = work.tile([P, C], F32, name="biased")
-                nc.vector.tensor_tensor(biased[:], z[jb][:], b_rows[:], ADD)
                 if jb == on_scalar:
-                    nc.scalar.activation(h[jb][:], biased[:], ACT.Relu, accum_out=h_sum[:])
+                    nc.scalar.activation(h[jb][:], z[jb][:], ACT.Relu, accum_out=h_sum[:])
                 else:
-                    nc.scalar.activation(h[jb][:], biased[:], ACT.Relu)
+                    nc.scalar.activation(h[jb][:], z[jb][:], ACT.Relu)
 
             unread_squares = work.tile([P, C], F32, name="unread_squares")
             square_sum = work.tile([P, 1], F32, name="square_sum")

@@ -11,7 +11,12 @@ FLOPS = 2 * F * C * N
 WARM_UP_MATMULS = 3
 
 BF16, F32, U16 = mybir.dt.bfloat16, mybir.dt.float32, mybir.dt.uint16
-ADD, SUBTRACT, MULT = mybir.AluOpType.add, mybir.AluOpType.subtract, mybir.AluOpType.mult
+ADD, SUBTRACT, MULT, MAX = (
+    mybir.AluOpType.add,
+    mybir.AluOpType.subtract,
+    mybir.AluOpType.mult,
+    mybir.AluOpType.max,
+)
 ACT = mybir.ActivationFunctionType
 
 
@@ -24,16 +29,16 @@ def tile_semanticgraphnetwork_kernel(tc, x, w, b, gain, beta, base, offs, out):
         tc.psum_pool(name="psum_t", bufs=3) as psum_t,
         tc.psum_pool(name="psum_once", bufs=1) as psum_once,
     ):
-        b_rows = held.tile([B_ROWS, C], F32, name="b_rows")
-        nc.sync.dma_start(b_rows[:], b.rearrange("c one -> (c one)").partition_broadcast(B_ROWS))
         x_sb = held.tile([P, FB, N], BF16, name="x_sb")
         w_sb = held.tile([P, FB, C], BF16, name="w_sb")
         x_view = x.rearrange("(p fb) j -> p fb j", fb=FB)
         w_view = w.rearrange("(p fb) c -> p fb c", fb=FB)
-        for half in range(2):
-            blocks = slice(half * FB // 2, (half + 1) * FB // 2)
+        b_rows = held.tile([B_ROWS, C], F32, name="b_rows")
+        for blocks in (slice(0, 1), slice(1, 2), slice(2, FB)):
             nc.sync.dma_start(x_sb[:, blocks, :], x_view[:, blocks, :])
             nc.scalar.dma_start(w_sb[:, blocks, :], w_view[:, blocks, :])
+            if blocks.start == 0:
+                nc.sync.dma_start(b_rows[:], b.rearrange("c one -> (c one)").partition_broadcast(B_ROWS))
 
         eps = held.tile([P, 1], F32, name="eps")
         nc.vector.memset(eps[:], LN_EPS)
@@ -63,6 +68,9 @@ def tile_semanticgraphnetwork_kernel(tc, x, w, b, gain, beta, base, offs, out):
         identity = held.tile([P, P], F32, name="identity")
         make_identity(nc, identity[:])
 
+        def upper_half(t):
+            return t.bitcast(BF16).rearrange("r (c half) -> r c half", half=2)[:, :, 1]
+
         minus_identity = held.tile([B_ROWS, B_ROWS], F32, name="minus_identity")
         nc.vector.tensor_scalar(minus_identity[:], identity[0:B_ROWS, 0:B_ROWS], -1.0, None, MULT)
         minus_from_row_1 = held.tile([B_ROWS, 1], F32, name="minus_from_row_1")
@@ -71,15 +79,11 @@ def tile_semanticgraphnetwork_kernel(tc, x, w, b, gain, beta, base, offs, out):
         ones = held.tile([P, P], BF16, name="ones")
         nc.vector.memset(ones[:], 0.0)
         nc.vector.memset(ones[0:B_TERMS, :], 1.0)
-        b_terms = held.tile([P, C], BF16, name="b_terms")
-        nc.vector.memset(b_terms[:], 0.0)
-        first = held.tile([B_ROWS, C], BF16, name="first")
-        nc.vector.tensor_copy(first[:], b_rows[:])
+        b_terms = held.tile([P, C], F32, name="b_terms")
+        nc.gpsimd.memset(b_terms[:], 0.0)
         rest = held.tile([B_ROWS, C], F32, name="rest")
-        nc.vector.scalar_tensor_tensor(rest[:], first[:], minus_from_row_1[:], b_rows[:], MULT, ADD)
-        second = held.tile([B_ROWS, C], BF16, name="second")
-        nc.vector.tensor_copy(second[:], rest[:])
-        nc.vector.scalar_tensor_tensor(b_terms[0:B_ROWS, :], second[:], minus_in_row_2, rest[:], MULT, ADD)
+        nc.vector.scalar_tensor_tensor(rest[:], upper_half(b_rows[:]), minus_from_row_1[:], b_rows[:], MULT, ADD)
+        nc.vector.scalar_tensor_tensor(b_terms[0:B_ROWS, :], upper_half(rest[:]), minus_in_row_2, rest[:], MULT, ADD)
 
         zeros = held.tile([P, N], F32, name="zeros")
         nc.gpsimd.memset(zeros[:], 0.0)
@@ -87,39 +91,53 @@ def tile_semanticgraphnetwork_kernel(tc, x, w, b, gain, beta, base, offs, out):
         for cb in range(CB):
             nc.gpsimd.tensor_scalar(beta_wide[cb][:], zeros[:], 1.0, beta_cols[:, cb : cb + 1], MULT, ADD)
 
-        z = []
-        for jb in range(JB):
-            z.append(psum_z.tile([P, C], F32, name="z"))
-            for fb in range(FB):
-                nc.tensor.matmul(
-                    z[jb][:], x_sb[:, fb, jb * P : (jb + 1) * P], w_sb[:, fb, :], start=(fb == 0), stop=False
-                )
-            nc.tensor.matmul(z[jb][:], ones[:], b_terms[:], start=False, stop=True)
+        z = [psum_z.tile([P, C], F32, name="z") for jb in range(JB)]
+
+        def multiply(jb, fb, start, stop):
+            nc.tensor.matmul(z[jb][:], x_sb[:, fb, jb * P : (jb + 1) * P], w_sb[:, fb, :], start=start, stop=stop)
+
+        def add_bias(jb, start, stop):
+            nc.tensor.matmul(z[jb][:], ones[:], upper_half(b_terms[:]), start=start, stop=stop)
+
+        for fb in range(FB // 2):
+            for jb in range(JB - 1):
+                multiply(jb, fb, start=(fb == 0), stop=False)
+        for jb in range(JB - 1):
+            add_bias(jb, start=False, stop=False)
+        for jb in range(JB - 1):
+            for fb in range(FB // 2, FB):
+                multiply(jb, fb, start=False, stop=(fb == FB - 1))
+        add_bias(JB - 1, start=True, stop=False)
+        for fb in range(FB):
+            multiply(JB - 1, fb, start=False, stop=(fb == FB - 1))
 
         h = [held.tile([P, C], F32, name=f"h{jb}") for jb in range(JB)]
         mean_var = [held.tile([P, 2], F32, name=f"mean_var{jb}") for jb in range(JB)]
         rstd = [held.tile([P, 1], F32, name=f"rstd{jb}") for jb in range(JB)]
-        for on_vector in range(0, JB, 2):
-            on_scalar = on_vector + 1
-            h_sum = work.tile([P, 1], F32, name="h_sum")
-            for jb in (on_vector, on_scalar):
-                if jb == on_scalar:
-                    nc.scalar.activation(h[jb][:], z[jb][:], ACT.Relu, accum_out=h_sum[:])
-                else:
-                    nc.scalar.activation(h[jb][:], z[jb][:], ACT.Relu)
 
+        def statistics_on_scalar(jb):
+            h_sum = work.tile([P, 1], F32, name="h_sum")
+            nc.scalar.activation(h[jb][:], z[jb][:], ACT.Relu, accum_out=h_sum[:])
+            nc.vector.tensor_scalar(mean_var[jb][:, 0:1], h_sum[:], 1.0 / C, None, MULT)
             unread_squares = work.tile([P, C], F32, name="unread_squares")
             square_sum = work.tile([P, 1], F32, name="square_sum")
             nc.scalar.activation(
-                unread_squares[:], h[on_scalar][:], ACT.Square, bias=h_sum[:], scale=-float(C), accum_out=square_sum[:]
+                unread_squares[:], h[jb][:], ACT.Square, bias=h_sum[:], scale=-float(C), accum_out=square_sum[:]
             )
-            six = work.tile([P, 6], F32, name="six")
-            nc.vector.bn_stats(six[:], h[on_vector][:])
-            nc.vector.bn_aggr(mean_var[on_vector][:], six[:])
-            nc.vector.tensor_scalar(mean_var[on_scalar][:, 0:1], h_sum[:], 1.0 / C, None, MULT)
+            nc.scalar.activation(rstd[jb][:], square_sum[:], ACT.Abs_reciprocal_sqrt, bias=eps[:], scale=1.0 / C**3)
 
-            nc.scalar.activation(rstd[on_vector][:], mean_var[on_vector][:, 1:2], ACT.Abs_reciprocal_sqrt, bias=eps[:])
-            nc.scalar.activation(rstd[on_scalar][:], square_sum[:], ACT.Abs_reciprocal_sqrt, bias=eps[:], scale=1.0 / C**3)
+        def statistics_on_vector(jb):
+            nc.vector.tensor_scalar(h[jb][:], z[jb][:], 0.0, None, MAX)
+            six = work.tile([P, 6], F32, name="six")
+            nc.vector.bn_stats(six[:], h[jb][:])
+            nc.vector.bn_aggr(mean_var[jb][:], six[:])
+            nc.scalar.activation(rstd[jb][:], mean_var[jb][:, 1:2], ACT.Abs_reciprocal_sqrt, bias=eps[:])
+
+        for jb in range(JB):
+            if jb in (0, JB - 1):
+                statistics_on_scalar(jb)
+            else:
+                statistics_on_vector(jb)
 
         normed = [held.tile([P, C], F32, name=f"normed{jb}") for jb in range(JB)]
         for jb in range(JB):

@@ -8,7 +8,7 @@ LN_EPS = 1e-5
 B_TERMS = 3
 B_ROWS = 4
 FLOPS = 2 * F * C * N
-WARM_UP_MATMULS = 3
+WARM_UP_MATMULS = 16
 
 BF16, F32, U16 = mybir.dt.bfloat16, mybir.dt.float32, mybir.dt.uint16
 ADD, SUBTRACT, MULT, MAX = (
@@ -29,6 +29,12 @@ def tile_semanticgraphnetwork_kernel(tc, x, w, b, gain, beta, base, offs, out):
         tc.psum_pool(name="psum_t", bufs=3) as psum_t,
         tc.psum_pool(name="psum_once", bufs=1) as psum_once,
     ):
+        cold = held.tile([P, P], BF16, name="cold")
+        nc.gpsimd.memset(cold[:], 0.0)
+        warm_out = psum_once.tile([P, P], F32, name="warm_out")
+        for repeat in range(WARM_UP_MATMULS):
+            nc.tensor.matmul(warm_out[:], cold[:], cold[:], start=True, stop=True)
+
         x_sb = held.tile([P, FB, N], BF16, name="x_sb")
         w_sb = held.tile([P, FB, C], BF16, name="w_sb")
         x_view = x.rearrange("(p fb) j -> p fb j", fb=FB)
@@ -58,12 +64,6 @@ def tile_semanticgraphnetwork_kernel(tc, x, w, b, gain, beta, base, offs, out):
         window = [held.tile([P, S], F32, name=f"window{cb}") for cb in range(CB)]
         for cb in range(CB):
             nc.sync.dma_start(window[cb][:], base_blocks[cb])
-
-        cold = held.tile([P, N], BF16, name="cold")
-        nc.vector.memset(cold[:], 0.0)
-        warm_out = psum_once.tile([P, N], F32, name="warm_out")
-        for repeat in range(WARM_UP_MATMULS):
-            nc.tensor.matmul(warm_out[:], cold[:, 0:P], cold[:], start=True, stop=True)
 
         identity = held.tile([P, P], F32, name="identity")
         make_identity(nc, identity[:])
@@ -140,25 +140,41 @@ def tile_semanticgraphnetwork_kernel(tc, x, w, b, gain, beta, base, offs, out):
                 statistics_on_vector(jb)
 
         normed = [held.tile([P, C], F32, name=f"normed{jb}") for jb in range(JB)]
+
+        def channel_block(t, cb):
+            return t[:].rearrange("j (p cb) -> j cb p", cb=CB)[:, cb, :]
+
+        last = JB - 1
+        centred = held.tile([P, P], F32, name="centred")
+        nc.vector.tensor_scalar(centred[:], channel_block(h[last], 0), mean_var[last][:, 0:1], None, SUBTRACT)
+        centred_flipped = psum_z.tile([P, P], F32, name="centred_flipped", tag="z")
+        nc.tensor.transpose(centred_flipped[:], centred[:], identity[:])
+        last_square = held.tile([P, P], F32, name="last_square")
+        nc.scalar.activation(last_square[:], centred_flipped[:], ACT.Identity, scale=gain_cols[:, 0:1])
+        rstd_rows = psum_z.tile([P, P], F32, name="rstd_rows", tag="z")
+        nc.tensor.transpose(rstd_rows[:], rstd[last][:].to_broadcast([P, P]), identity[:])
+
         for jb in range(JB):
             nc.vector.tensor_scalar(normed[jb][:], h[jb][:], mean_var[jb][:, 0:1], rstd[jb][:], SUBTRACT, MULT)
-
-        def channel_block(jb, cb):
-            return normed[jb][:].rearrange("j (p cb) -> j cb p", cb=CB)[:, cb, :]
 
         for cb in range(CB):
             scaled = work.tile([P, N], F32, name="scaled")
             if cb == 0:
-                for jb in range(JB):
+                for jb in range(last):
                     square = psum_t.tile([P, P], F32, name="square", tag="bank")
-                    nc.tensor.transpose(square[:], channel_block(jb, 0), identity[:])
+                    nc.tensor.transpose(square[:], channel_block(normed[jb], 0), identity[:])
                     nc.scalar.activation(
                         scaled[:, jb * P : (jb + 1) * P], square[:], ACT.Identity, scale=gain_cols[:, 0:1]
                     )
+                nc.vector.tensor_tensor(scaled[:, last * P : N], last_square[:], rstd_rows[:], MULT)
             else:
                 flipped = psum_t.tile([P, N], F32, name="flipped", tag="bank")
                 for jb in range(JB):
-                    nc.tensor.transpose(flipped[:, jb * P : (jb + 1) * P], channel_block(jb, cb), identity[:])
+                    nc.tensor.transpose(flipped[:, jb * P : (jb + 1) * P], channel_block(normed[jb], cb), identity[:])
                 nc.scalar.activation(scaled[:], flipped[:], ACT.Identity, scale=gain_cols[:, cb : cb + 1])
             nc.vector.tensor_tensor(window[cb][:].indirect(offsets[:]), scaled[:], beta_wide[cb][:], ADD)
-            nc.sync.dma_start(out_blocks[cb], window[cb][:])
+            if cb < CB - 1:
+                nc.sync.dma_start(out_blocks[cb], window[cb][:])
+            else:
+                nc.sync.dma_start(out_blocks[cb][:, 0 : S // 2], window[cb][:, 0 : S // 2])
+                nc.scalar.dma_start(out_blocks[cb][:, S // 2 : S], window[cb][:, S // 2 : S])

@@ -163,9 +163,11 @@ def tile_semanticgraphnetwork_kernel(tc, x, w, b, gain, beta, base, offs, out):
                 for jb in range(last):
                     square = psum_t.tile([P, P], F32, name="square", tag="bank")
                     nc.tensor.transpose(square[:], channel_block(normed[jb], 0), identity[:])
-                    nc.scalar.activation(
-                        scaled[:, jb * P : (jb + 1) * P], square[:], ACT.Identity, scale=gain_cols[:, 0:1]
-                    )
+                    columns = scaled[:, jb * P : (jb + 1) * P]
+                    if jb == 0:
+                        nc.vector.tensor_scalar(columns, square[:], gain_cols[:, 0:1], None, MULT)
+                    else:
+                        nc.scalar.activation(columns, square[:], ACT.Identity, scale=gain_cols[:, 0:1])
                 nc.vector.tensor_tensor(scaled[:, last * P : N], last_square[:], rstd_rows[:], MULT)
             else:
                 flipped = psum_t.tile([P, N], F32, name="flipped", tag="bank")

import concourse.mybir as mybir
from concourse.masks import make_identity

P = 128
F, C, S, N = 512, 512, 2048, 512
FB, CB, JB = F // P, C // P, N // P
LN_EPS = 1e-5
B_TERMS = 3
B_ROWS = 4
FLOPS = 2 * F * C * N
WARM_UP_MATMULS = 16

BF16, F32, U16 = mybir.dt.bfloat16, mybir.dt.float32, mybir.dt.uint16
ADD, SUBTRACT, MULT, MAX = (
    mybir.AluOpType.add,
    mybir.AluOpType.subtract,
    mybir.AluOpType.mult,
    mybir.AluOpType.max,
)
ACT = mybir.ActivationFunctionType


def tile_semanticgraphnetwork_kernel(tc, x, w, b, gain, beta, base, offs, out):
    nc = tc.nc
    with (
        tc.tile_pool(name="held", bufs=1) as held,
        tc.tile_pool(name="work", bufs=2) as work,
        tc.psum_pool(name="psum_z", bufs=JB) as psum_z,
        tc.psum_pool(name="psum_t", bufs=3) as psum_t,
        tc.psum_pool(name="psum_once", bufs=1) as psum_once,
    ):
        cold = held.tile([P, P], BF16, name="cold")
        nc.gpsimd.memset(cold[:], 0.0)
        warm_out = psum_once.tile([P, P], F32, name="warm_out")
        for repeat in range(WARM_UP_MATMULS):
            nc.tensor.matmul(warm_out[:], cold[:], cold[:], start=True, stop=True)

        x_sb = held.tile([P, FB, N], BF16, name="x_sb")
        w_sb = held.tile([P, FB, C], BF16, name="w_sb")
        x_view = x.rearrange("(p fb) j -> p fb j", fb=FB)
        w_view = w.rearrange("(p fb) c -> p fb c", fb=FB)
        b_rows = held.tile([B_ROWS, C], F32, name="b_rows")
        for blocks in (slice(0, 1), slice(1, 2), slice(2, FB)):
            nc.sync.dma_start(x_sb[:, blocks, :], x_view[:, blocks, :])
            nc.scalar.dma_start(w_sb[:, blocks, :], w_view[:, blocks, :])
            if blocks.start == 0:
                nc.sync.dma_start(b_rows[:], b.rearrange("c one -> (c one)").partition_broadcast(B_ROWS))

        eps = held.tile([P, 1], F32, name="eps")
        nc.vector.memset(eps[:], LN_EPS)
        unread = held.tile([P, 1], F32, name="unread")
        nc.scalar.activation(unread[:], eps[:], ACT.Abs_reciprocal_sqrt)

        offsets = held.tile([P, N // 16], U16, name="offsets")
        nc.sync.dma_start(offsets[:], offs)

        gain_cols = held.tile([P, CB], F32, name="gain_cols")
        beta_cols = held.tile([P, CB], F32, name="beta_cols")
        nc.scalar.dma_start(beta_cols[:], beta.rearrange("(p cb) one -> p (cb one)", cb=CB))
        nc.scalar.dma_start(gain_cols[:], gain.rearrange("(p cb) one -> p (cb one)", cb=CB))

        base_blocks = base.rearrange("(p cb) s -> cb p s", cb=CB)
        out_blocks = out.rearrange("(p cb) s -> cb p s", cb=CB)
        window = [held.tile([P, S], F32, name=f"window{cb}") for cb in range(CB)]
        for cb in range(CB):
            nc.sync.dma_start(window[cb][:], base_blocks[cb])

        identity = held.tile([P, P], F32, name="identity")
        make_identity(nc, identity[:])

        def upper_half(t):
            return t.bitcast(BF16).rearrange("r (c half) -> r c half", half=2)[:, :, 1]

        minus_identity = held.tile([B_ROWS, B_ROWS], F32, name="minus_identity")
        nc.vector.tensor_scalar(minus_identity[:], identity[0:B_ROWS, 0:B_ROWS], -1.0, None, MULT)
        minus_from_row_1 = held.tile([B_ROWS, 1], F32, name="minus_from_row_1")
        nc.vector.tensor_scalar(minus_from_row_1[:], identity[0:B_ROWS, 0:1], 1.0, None, SUBTRACT)
        minus_in_row_2 = minus_identity[:, 2:3]
        ones = held.tile([P, P], BF16, name="ones")
        nc.vector.memset(ones[:], 0.0)
        nc.vector.memset(ones[0:B_TERMS, :], 1.0)
        b_terms = held.tile([P, C], F32, name="b_terms")
        nc.gpsimd.memset(b_terms[:], 0.0)
        rest = held.tile([B_ROWS, C], F32, name="rest")
        nc.vector.scalar_tensor_tensor(rest[:], upper_half(b_rows[:]), minus_from_row_1[:], b_rows[:], MULT, ADD)
        nc.vector.scalar_tensor_tensor(b_terms[0:B_ROWS, :], upper_half(rest[:]), minus_in_row_2, rest[:], MULT, ADD)

        zeros = held.tile([P, N], F32, name="zeros")
        nc.gpsimd.memset(zeros[:], 0.0)
        beta_wide = [held.tile([P, N], F32, name=f"beta_wide{cb}") for cb in range(CB)]
        for cb in range(CB):
            nc.gpsimd.tensor_scalar(beta_wide[cb][:], zeros[:], 1.0, beta_cols[:, cb : cb + 1], MULT, ADD)

        z = [psum_z.tile([P, C], F32, name="z") for jb in range(JB)]

        def multiply(jb, fb, start, stop):
            nc.tensor.matmul(z[jb][:], x_sb[:, fb, jb * P : (jb + 1) * P], w_sb[:, fb, :], start=start, stop=stop)

        def add_bias(jb, start, stop):
            nc.tensor.matmul(z[jb][:], ones[:], upper_half(b_terms[:]), start=start, stop=stop)

        for fb in range(FB // 2):
            for jb in range(JB - 1):
                multiply(jb, fb, start=(fb == 0), stop=False)
        for jb in range(JB - 1):
            add_bias(jb, start=False, stop=False)
        for jb in range(JB - 1):
            for fb in range(FB // 2, FB):
                multiply(jb, fb, start=False, stop=(fb == FB - 1))
        add_bias(JB - 1, start=True, stop=False)
        for fb in range(FB):
            multiply(JB - 1, fb, start=False, stop=(fb == FB - 1))

        h = [held.tile([P, C], F32, name=f"h{jb}") for jb in range(JB)]
        mean_var = [held.tile([P, 2], F32, name=f"mean_var{jb}") for jb in range(JB)]
        rstd = [held.tile([P, 1], F32, name=f"rstd{jb}") for jb in range(JB)]

        def statistics_on_scalar(jb):
            h_sum = work.tile([P, 1], F32, name="h_sum")
            nc.scalar.activation(h[jb][:], z[jb][:], ACT.Relu, accum_out=h_sum[:])
            nc.vector.tensor_scalar(mean_var[jb][:, 0:1], h_sum[:], 1.0 / C, None, MULT)
            unread_squares = work.tile([P, C], F32, name="unread_squares")
            square_sum = work.tile([P, 1], F32, name="square_sum")
            nc.scalar.activation(
                unread_squares[:], h[jb][:], ACT.Square, bias=h_sum[:], scale=-float(C), accum_out=square_sum[:]
            )
            nc.scalar.activation(rstd[jb][:], square_sum[:], ACT.Abs_reciprocal_sqrt, bias=eps[:], scale=1.0 / C**3)

        def statistics_on_vector(jb):
            nc.vector.tensor_scalar(h[jb][:], z[jb][:], 0.0, None, MAX)
            six = work.tile([P, 6], F32, name="six")
            nc.vector.bn_stats(six[:], h[jb][:])
            nc.vector.bn_aggr(mean_var[jb][:], six[:])
            nc.scalar.activation(rstd[jb][:], mean_var[jb][:, 1:2], ACT.Abs_reciprocal_sqrt, bias=eps[:])

        for jb in range(JB):
            if jb in (0, JB - 1):
                statistics_on_scalar(jb)
            else:
                statistics_on_vector(jb)

        normed = [held.tile([P, C], F32, name=f"normed{jb}") for jb in range(JB)]

        def channel_block(t, cb):
            return t[:].rearrange("j (p cb) -> j cb p", cb=CB)[:, cb, :]

        last = JB - 1
        centred = held.tile([P, P], F32, name="centred")
        nc.vector.tensor_scalar(centred[:], channel_block(h[last], 0), mean_var[last][:, 0:1], None, SUBTRACT)
        centred_flipped = psum_z.tile([P, P], F32, name="centred_flipped", tag="z")
        nc.tensor.transpose(centred_flipped[:], centred[:], identity[:])
        last_square = held.tile([P, P], F32, name="last_square")
        nc.scalar.activation(last_square[:], centred_flipped[:], ACT.Identity, scale=gain_cols[:, 0:1])
        rstd_rows = psum_z.tile([P, P], F32, name="rstd_rows", tag="z")
        nc.tensor.transpose(rstd_rows[:], rstd[last][:].to_broadcast([P, P]), identity[:])

        for jb in range(JB):
            nc.vector.tensor_scalar(normed[jb][:], h[jb][:], mean_var[jb][:, 0:1], rstd[jb][:], SUBTRACT, MULT)

        for cb in range(CB):
            scaled = work.tile([P, N], F32, name="scaled")
            if cb == 0:
                for jb in range(last):
                    square = psum_t.tile([P, P], F32, name="square", tag="bank")
                    nc.tensor.transpose(square[:], channel_block(normed[jb], 0), identity[:])
                    columns = scaled[:, jb * P : (jb + 1) * P]
                    if jb == 0:
                        nc.vector.tensor_scalar(columns, square[:], gain_cols[:, 0:1], None, MULT)
                    else:
                        nc.scalar.activation(columns, square[:], ACT.Identity, scale=gain_cols[:, 0:1])
                nc.vector.tensor_tensor(scaled[:, last * P : N], last_square[:], rstd_rows[:], MULT)
            else:
                flipped = psum_t.tile([P, N], F32, name="flipped", tag="bank")
                for jb in range(JB):
                    nc.tensor.transpose(flipped[:, jb * P : (jb + 1) * P], channel_block(normed[jb], cb), identity[:])
                nc.scalar.activation(scaled[:], flipped[:], ACT.Identity, scale=gain_cols[:, cb : cb + 1])
            nc.vector.tensor_tensor(window[cb][:].indirect(offsets[:]), scaled[:], beta_wide[cb][:], ADD)
            if cb < CB - 1:
                nc.sync.dma_start(out_blocks[cb], window[cb][:])
            else:
                nc.sync.dma_start(out_blocks[cb][:, 0 : S // 2], window[cb][:, 0 : S // 2])
                nc.scalar.dma_start(out_blocks[cb][:, S // 2 : S], window[cb][:, S // 2 : S])
